import numpy as np
import ml_dtypes


def mxq(x, axis, fmt="e4m3"):
    dtype, down = {"e4m3": (ml_dtypes.float8_e4m3fn, 7), "e5m2": (ml_dtypes.float8_e5m2, 14)}[fmt]
    v = np.moveaxis(np.asarray(x, np.float32).astype(ml_dtypes.bfloat16).astype(np.float64), axis, -1)
    blocks = v.reshape(v.shape[:-1] + (-1, 32))
    amax = np.abs(blocks).max(-1, keepdims=True)
    byte = np.maximum(np.where(amax > 0, np.frexp(amax)[1] - 1 + 127, 0) - down, 1)
    scale = np.exp2(byte - 127.0)
    codes = (blocks / scale).astype(np.float32).astype(dtype).astype(np.float64)
    return np.moveaxis((codes * scale).reshape(v.shape), -1, axis)


WIDE = False


def mx_kscale(k):
    if not WIDE:
        return np.ones(k)
    levels = np.array([10, -10, 5, -5, 0])
    a = np.random.permutation(np.resize(levels, k // 512 * 4)).reshape(k // 512, 4)
    idx = np.arange(k)
    return np.exp2(a[idx // 512, idx % 128 // 32])


BF16 = ml_dtypes.bfloat16


def bf(x):
    return np.asarray(x, np.float32).astype(BF16)


def f64(x):
    return np.asarray(x).astype(np.float64)


B, S, D, F1, F2, F3, F4 = 512, 16, 256, 512, 128, 1024, 512
K = D + D


def setup_inputs():
    s, t = mx_kscale(K), mx_kscale(F1)
    return {"x1": bf(np.random.standard_normal((B, S, D)) * s[:D]),
            "x2": bf(np.random.standard_normal((B, S, D)) * s[D:]),
            "W1": bf(np.random.standard_normal((S, K, F1)) * 1.0 / np.sqrt(K) / s[None, :, None] * t[None, None, :]),
            "b1": bf(np.random.standard_normal((S, F1)) * 0.3 * t),
            "W2": bf(np.random.standard_normal((S, F1, F2)) * 1.4 / np.sqrt(F1) / t[None, :, None]),
            "b2": bf(np.random.standard_normal((S, F2)) * 0.3)}


def reference(x1, x2, W1, b1, W2, b2):
    x = np.concatenate([f64(x1), f64(x2)], axis=-1).transpose(1, 0, 2)
    h = np.maximum((mxq(x, 2, "e4m3") @ mxq(f64(W1), 1, "e4m3")) + f64(b1)[:, None, :], 0.0)
    y = (mxq(h, 2, "e4m3") @ mxq(f64(W2), 1, "e4m3")) + f64(b2)[:, None, :]
    return y.transpose(1, 0, 2)

@@ -1,0 +1,282 @@
+from contextlib import ExitStack
+
+import concourse.bass as bass
+import concourse.mybir as mybir
+import concourse.tile as tile
+from concourse.masks import make_identity
+
+F32 = mybir.dt.float32
+BF16 = mybir.dt.bfloat16
+I32 = mybir.dt.int32
+U32 = mybir.dt.uint32
+U8 = mybir.dt.uint8
+FP8X4 = mybir.dt.float8_e4m3fn_x4
+RELU = mybir.ActivationFunctionType.Relu
+ADD = mybir.AluOpType.add
+
+P = 128
+B, S, D, F1, F2 = 512, 16, 256, 512, 128
+K = 2 * D
+FLOPS = 2 * S * B * K * F1 + 2 * S * B * F1 * F2
+
+MANUAL = False
+W1_S_COLS = 256
+G = 4
+STORES = ((0, 4), (4, 4), (8, 4), (12, 2), (14, 1), (15, 1))
+
+
+def tile_simplefusionmodule_pa_t_kernel(tc, x1, x2, W1, b1, W2, b2, out):
+    nc = tc.nc
+    with ExitStack() as ctx:
+        const = ctx.enter_context(tc.tile_pool(name="const", bufs=1))
+        xpool = ctx.enter_context(tc.tile_pool(name="xpool", bufs=4))
+        w1pool = ctx.enter_context(tc.tile_pool(name="w1pool", bufs=6))
+        work = ctx.enter_context(tc.tile_pool(name="work", bufs=2))
+        ps_x = ctx.enter_context(tc.psum_pool(name="ps_x", bufs=2))
+        ps_h = ctx.enter_context(tc.psum_pool(name="ps_h", bufs=4))
+        ps_o = ctx.enter_context(tc.psum_pool(name="ps_o", bufs=2))
+        if MANUAL:
+            ctx.enter_context(tc.manual_schedule())
+
+        b1r = const.tile([P, P], BF16, name="b1r")
+        nc.vector.memset(b1r[:].bitcast(I32), 0)
+        nc.scalar.dma_start(out=b1r[0:64, :], in_=b1.rearrange("s (t p) -> (s t) p", p=P))
+        b2z = const.tile([P, S * F2], BF16, name="b2z")
+        nc.vector.memset(b2z[:].bitcast(I32), 0)
+        nc.scalar.dma_start(out=b2z[0:1, :], in_=b2.rearrange("(o s) f -> o (s f)", o=1))
+        ident_f = const.tile([P, P], F32, name="ident_f")
+        make_identity(nc, ident_f[:])
+        ident_b = const.tile([P, P], BF16, name="ident_b")
+        make_identity(nc, ident_b[:])
+        ones_b = const.tile([P, P], BF16, name="ones_b")
+        nc.gpsimd.memset(ones_b[:], 1.0)
+
+        x1v = x1.rearrange("(p j) s d -> p j s d", j=4)
+        x2v = x2.rearrange("(p j) s d -> p j s d", j=4)
+        xt = {}
+        w1raw = {}
+        w2raw = const.tile([P, G, 4, G * F2], BF16, name="w2raw")
+
+        def alloc_x(g):
+            xa = xpool.tile([P, 4, G, D], BF16, name="x1t", tag="x1t")
+            xb = xpool.tile([P, 4, G, D], BF16, name="x2t", tag="x2t")
+            xt[g] = (xa, xb)
+
+        def load_x_style(s):
+            g, sl = divmod(s, G)
+            nc.sync.dma_start(out=xt[g][0][:, :, sl, :], in_=x1v[:, :, s, :])
+            nc.sync.dma_start(out=xt[g][1][:, :, sl, :], in_=x2v[:, :, s, :])
+
+        def load_x_group(g):
+            nc.sync.dma_start(out=xt[g][0][:], in_=x1v[:, :, g * G : (g + 1) * G, :])
+            nc.sync.dma_start(out=xt[g][1][:], in_=x2v[:, :, g * G : (g + 1) * G, :])
+
+        def alloc_w1(h):
+            w1raw[h] = w1pool.tile([P, 2, 2, 2 * F1], BF16, name="w1raw", tag="w1raw")
+
+        def load_w1(s0, n):
+            h, sl = divmod(s0, 2)
+            nc.sync.dma_start(
+                out=w1raw[h][:, sl : sl + n, :, :],
+                in_=W1[s0 : s0 + n].rearrange("s (u p e) c -> p s u (e c)", u=2, p=P, e=2),
+            )
+
+        def load_w2(q):
+            for t in range(4):
+                nc.sync.dma_start(
+                    out=w2raw[:, q, t, :].rearrange("p (s c) -> p s c", s=G),
+                    in_=W2[q * G : (q + 1) * G, t * P : (t + 1) * P, :].rearrange("s p c -> p s c"),
+                )
+
+        alloc_x(0)
+        alloc_w1(0)
+        alloc_w1(1)
+        load_w1(0, 1)
+        load_x_style(0)
+        load_w1(1, 1)
+        load_x_style(1)
+        load_w2(0)
+        load_w1(2, 1)
+        load_x_style(2)
+        load_w1(3, 1)
+        load_x_style(3)
+        for g in range(1, 4):
+            alloc_x(g)
+            load_x_group(g)
+            alloc_w1(2 * g)
+            load_w1(4 * g, 2)
+            alloc_w1(2 * g + 1)
+            load_w1(4 * g + 2, 2)
+            load_w2(g)
+
+        pt = ps_o.tile([P, P], BF16, name="pt", tag="ob")
+        nc.tensor.transpose(pt[:], b1r[:], ident_b[:])
+        b1T = const.tile([P, 64], F32, name="b1T")
+        nc.vector.tensor_copy(out=b1T[:], in_=pt[:, 0:64])
+        b2b = const.tile([P, S * F2], F32, name="b2b")
+        for i in range(4):
+            pb = ps_h.tile([P, 512], F32, name="pb", tag="hb")
+            nc.tensor.matmul(pb[:], lhsT=ones_b[:], rhs=b2z[:, i * 512 : (i + 1) * 512], start=True, stop=True)
+            if i % 2 == 0:
+                nc.vector.tensor_copy(out=b2b[:, i * 512 : (i + 1) * 512], in_=pb[:])
+            else:
+                nc.scalar.copy(out=b2b[:, i * 512 : (i + 1) * 512], in_=pb[:])
+
+        w2c = const.tile([P, S * F2], U32, name="w2c", align_bytes=64)
+        w2s = const.tile([P, S * F2], U8, name="w2s", align_bytes=64)
+
+        xT, xg, xc, xs = {}, {}, {}, {}
+        w1g, w1c, w1s = {}, {}, {}
+        hb, hp, hg, hc, hs = {}, {}, {}, {}, {}
+        ob, osb, w2g = {}, {}, {}
+
+        def regroup(eng_copy, dst, src, c0, c1):
+            eng_copy(
+                out=dst[:, c0:c1, :].rearrange("p (c i) t -> p c t i", i=4),
+                in_=src[:, :, c0:c1].rearrange("p t (c i) -> p c t i", i=4),
+            )
+
+        def w1_src(s):
+            h, sl = divmod(s, 2)
+            return w1raw[h][:, sl, :, :].rearrange("p u (e c) -> p (u e) c", e=2)
+
+        def regroup_w1_s(s):
+            w1g[s] = work.tile([P, F1, 4], BF16, name="w1g", tag="w1g", align_bytes=64)
+            if W1_S_COLS > 0:
+                regroup(nc.scalar.copy, w1g[s], w1_src(s), F1 - W1_S_COLS, F1)
+
+        def regroup_w1_v(s):
+            regroup(nc.vector.tensor_copy, w1g[s], w1_src(s), 0, F1 - W1_S_COLS)
+
+        def quant_w1(s):
+            w1c[s] = work.tile([P, F1], U32, name="w1c", tag="w1c", bufs=3, align_bytes=64)
+            w1s[s] = work.tile([P, F1], U8, name="w1s", tag="w1s", bufs=3, align_bytes=64)
+            nc.vector.quantize_mx(
+                out=w1c[s][:].bitcast(FP8X4), scales=w1s[s][:], in_=w1g[s][:].rearrange("p c t -> p (c t)")
+            )
+
+        def transposes(s):
+            g, sl = divmod(s, G)
+            xT[s] = []
+            for jh in range(2):
+                bank = ps_x.tile([P, 2, 256], F32, name="xT", tag="xT")
+                xT[s].append(bank)
+                for u in range(2):
+                    xf = xt[g][u][:].rearrange("p j s d -> p (j s d)").bitcast(F32)
+                    for jl in range(2):
+                        col = ((2 * jh + jl) * G + sl) * P
+                        nc.tensor.transpose(bank[:, u, jl * P : (jl + 1) * P], xf[:, col : col + P], ident_f[:])
+
+        def evac_x(s):
+            xg[s] = work.tile([P, 4 * B], BF16, name="xg", tag="xg", align_bytes=64)
+            xgf = xg[s][:].bitcast(F32).rearrange("p (c u) -> p c u", u=2)
+            for jh in range(2):
+                nc.scalar.copy(out=xgf[:, jh * 256 : (jh + 1) * 256, :], in_=xT[s][jh][:].rearrange("p u c -> p c u"))
+
+        def quant_x(s):
+            xc[s] = work.tile([P, B], U32, name="xc", tag="xc", align_bytes=64)
+            xs[s] = work.tile([P, B], U8, name="xs", tag="xs", align_bytes=64)
+            nc.vector.quantize_mx(out=xc[s][:].bitcast(FP8X4), scales=xs[s][:], in_=xg[s][:])
+
+        def layer1(s):
+            hb[s] = []
+            for t in range(4):
+                bank = ps_h.tile([P, B], F32, name="hb", tag="hb")
+                hb[s].append(bank)
+                nc.tensor.matmul_mx(
+                    out=bank[:],
+                    lhsT=w1c[s][:, t * P : (t + 1) * P].bitcast(FP8X4),
+                    lhsT_scale=w1s[s][:, t * P : (t + 1) * P],
+                    rhs=xc[s][:].bitcast(FP8X4),
+                    rhs_scale=xs[s][:],
+                    start=True,
+                    stop=True,
+                )
+
+        def evac_h(s):
+            hp[s] = work.tile([P, 4, B], BF16, name="hp", tag="hp")
+            for t in range(4):
+                nc.scalar.activation(
+                    out=hp[s][:, t, :], in_=hb[s][t][:], func=RELU, bias=b1T[:, 4 * s + t : 4 * s + t + 1], scale=1.0
+                )
+
+        def regroup_h(s):
+            hg[s] = work.tile([P, B, 4], BF16, name="hg", tag="hg", align_bytes=64)
+            regroup(nc.vector.tensor_copy, hg[s], hp[s], 0, B)
+
+        def quant_h(s):
+            hc[s] = work.tile([P, B], U32, name="hc", tag="hc", align_bytes=64)
+            hs[s] = work.tile([P, B], U8, name="hs", tag="hs", align_bytes=64)
+            nc.vector.quantize_mx(
+                out=hc[s][:].bitcast(FP8X4), scales=hs[s][:], in_=hg[s][:].rearrange("p c t -> p (c t)")
+            )
+
+        def regroup_w2(q):
+            w2g[q] = work.tile([P, G * F2, 4], BF16, name="w2g", tag="w2g", bufs=1, align_bytes=64)
+            regroup(nc.vector.tensor_copy, w2g[q], w2raw[:, q, :, :], 0, G * F2)
+
+        def quant_w2(q):
+            cols = slice(q * G * F2, (q + 1) * G * F2)
+            nc.vector.quantize_mx(
+                out=w2c[:, cols].bitcast(FP8X4), scales=w2s[:, cols], in_=w2g[q][:].rearrange("p c t -> p (c t)")
+            )
+
+        def layer2(s):
+            ob[s] = ps_o.tile([P, 4, F2], F32, name="ob", tag="ob")
+            for j in range(4):
+                nc.tensor.matmul_mx(
+                    out=ob[s][:, j, :],
+                    lhsT=hc[s][:, j * P : (j + 1) * P].bitcast(FP8X4),
+                    lhsT_scale=hs[s][:, j * P : (j + 1) * P],
+                    rhs=w2c[:, s * F2 : (s + 1) * F2].bitcast(FP8X4),
+                    rhs_scale=w2s[:, s * F2 : (s + 1) * F2],
+                    start=True,
+                    stop=True,
+                )
+
+        outv = out.rearrange("(p j) s f -> p j s f", j=4)
+
+        def evac_o(s):
+            g, sl = divmod(s, G)
+            if sl == 0:
+                osb[g] = work.tile([P, 4, G, F2], F32, name="osb", tag="osb")
+            nc.vector.tensor_tensor(
+                out=osb[g][:, :, sl, :],
+                in0=ob[s][:],
+                in1=b2b[:, s * F2 : (s + 1) * F2].unsqueeze(1).to_broadcast([P, 4, F2]),
+                op=ADD,
+            )
+            for s0, n in STORES:
+                if s0 + n - 1 == s:
+                    nc.sync.dma_start(out=outv[:, :, s0 : s0 + n, :], in_=osb[g][:, :, s0 - g * G : s0 - g * G + n, :])
+
+        def on(s):
+            return 0 <= s < S
+
+        for k in range(-3, S + 2):
+            if on(k + 2):
+                transposes(k + 2)
+            if on(k - 1):
+                layer2(k - 1)
+            if on(k):
+                evac_h(k)
+            if on(k + 2):
+                regroup_w1_v(k + 2)
+            if on(k + 1):
+                quant_x(k + 1)
+                layer1(k + 1)
+            if on(k + 1) and (k + 1) % G == 0:
+                regroup_w2((k + 1) // G)
+            if on(k + 2):
+                quant_w1(k + 2)
+                evac_x(k + 2)
+            if on(k + 3):
+                regroup_w1_s(k + 3)
+            if on(k + 1) and (k + 1) % G == 0:
+                quant_w2((k + 1) // G)
+            if on(k):
+                regroup_h(k)
+            if on(k - 1):
+                evac_o(k - 1)
+            if on(k):
+                quant_h(k)

@@ -19,18 +19,21 @@ B, S, D, F1, F2 = 512, 16, 256, 512, 128
 K = 2 * D
 FLOPS = 2 * S * B * K * F1 + 2 * S * B * F1 * F2
 
-MANUAL = False
+MANUAL = True
 W1_S_COLS = 256
+W1_S_COLS_FIRST = 128
+LAST = 15
+OSB_BUFS = {4: 2, 2: 1, 1: 3}
 G = 4
-STORES = ((0, 4), (4, 4), (8, 4), (12, 2), (14, 1), (15, 1))
+STORES = ((0, 4), (4, 4), (8, 4), (12, 2), (14, 1))
 
 
 def tile_simplefusionmodule_pa_t_kernel(tc, x1, x2, W1, b1, W2, b2, out):
     nc = tc.nc
     with ExitStack() as ctx:
         const = ctx.enter_context(tc.tile_pool(name="const", bufs=1))
-        xpool = ctx.enter_context(tc.tile_pool(name="xpool", bufs=4))
-        w1pool = ctx.enter_context(tc.tile_pool(name="w1pool", bufs=6))
+        xpool = ctx.enter_context(tc.tile_pool(name="xpool", bufs=1))
+        w1pool = ctx.enter_context(tc.tile_pool(name="w1pool", bufs=5))
         work = ctx.enter_context(tc.tile_pool(name="work", bufs=2))
         ps_x = ctx.enter_context(tc.psum_pool(name="ps_x", bufs=2))
         ps_h = ctx.enter_context(tc.psum_pool(name="ps_h", bufs=4))
@@ -40,10 +43,10 @@ def tile_simplefusionmodule_pa_t_kernel(tc, x1, x2, W1, b1, W2, b2, out):
 
         b1r = const.tile([P, P], BF16, name="b1r")
         nc.vector.memset(b1r[:].bitcast(I32), 0)
-        nc.scalar.dma_start(out=b1r[0:64, :], in_=b1.rearrange("s (t p) -> (s t) p", p=P))
+        nc.sync.dma_start(out=b1r[0:64, :], in_=b1.rearrange("s (t p) -> (s t) p", p=P))
         b2z = const.tile([P, S * F2], BF16, name="b2z")
         nc.vector.memset(b2z[:].bitcast(I32), 0)
-        nc.scalar.dma_start(out=b2z[0:1, :], in_=b2.rearrange("(o s) f -> o (s f)", o=1))
+        nc.sync.dma_start(out=b2z[0:1, :], in_=b2.rearrange("(o s) f -> o (s f)", o=1))
         ident_f = const.tile([P, P], F32, name="ident_f")
         make_identity(nc, ident_f[:])
         ident_b = const.tile([P, P], BF16, name="ident_b")
@@ -57,19 +60,13 @@ def tile_simplefusionmodule_pa_t_kernel(tc, x1, x2, W1, b1, W2, b2, out):
         w1raw = {}
         w2raw = const.tile([P, G, 4, G * F2], BF16, name="w2raw")
 
-        def alloc_x(g):
-            xa = xpool.tile([P, 4, G, D], BF16, name="x1t", tag="x1t")
-            xb = xpool.tile([P, 4, G, D], BF16, name="x2t", tag="x2t")
-            xt[g] = (xa, xb)
-
-        def load_x_style(s):
-            g, sl = divmod(s, G)
-            nc.sync.dma_start(out=xt[g][0][:, :, sl, :], in_=x1v[:, :, s, :])
-            nc.sync.dma_start(out=xt[g][1][:, :, sl, :], in_=x2v[:, :, s, :])
-
-        def load_x_group(g):
-            nc.sync.dma_start(out=xt[g][0][:], in_=x1v[:, :, g * G : (g + 1) * G, :])
-            nc.sync.dma_start(out=xt[g][1][:], in_=x2v[:, :, g * G : (g + 1) * G, :])
+        def load_x_styles(s, n):
+            xa = xpool.tile([P, 4, n, D], BF16, name="x1t%d" % s)
+            xb = xpool.tile([P, 4, n, D], BF16, name="x2t%d" % s)
+            nc.sync.dma_start(out=xa[:], in_=x1v[:, :, s : s + n, :])
+            nc.sync.dma_start(out=xb[:], in_=x2v[:, :, s : s + n, :])
+            for i in range(n):
+                xt[s + i] = (xa, xb, i, n)
 
         def alloc_w1(h):
             w1raw[h] = w1pool.tile([P, 2, 2, 2 * F1], BF16, name="w1raw", tag="w1raw")
@@ -88,26 +85,30 @@ def tile_simplefusionmodule_pa_t_kernel(tc, x1, x2, W1, b1, W2, b2, out):
                     in_=W2[q * G : (q + 1) * G, t * P : (t + 1) * P, :].rearrange("s p c -> p s c"),
                 )
 
-        alloc_x(0)
         alloc_w1(0)
         alloc_w1(1)
-        load_w1(0, 1)
-        load_x_style(0)
-        load_w1(1, 1)
-        load_x_style(1)
+        for s in range(3):
+            load_x_styles(s, 1)
+            load_w1(s, 1)
         load_w2(0)
-        load_w1(2, 1)
-        load_x_style(2)
+        load_x_styles(3, 1)
         load_w1(3, 1)
-        load_x_style(3)
-        for g in range(1, 4):
-            alloc_x(g)
-            load_x_group(g)
-            alloc_w1(2 * g)
-            load_w1(4 * g, 2)
-            alloc_w1(2 * g + 1)
-            load_w1(4 * g + 2, 2)
-            load_w2(g)
+        for s in (4, 6):
+            load_x_styles(s, 2)
+            alloc_w1(s // 2)
+            load_w1(s, 1)
+            load_w1(s + 1, 1)
+        load_w2(1)
+        for s in (8, 10):
+            load_x_styles(s, 2)
+            alloc_w1(s // 2)
+            load_w1(s, 2)
+        load_w2(2)
+        load_x_styles(12, 4)
+        for s in (12, 14):
+            alloc_w1(s // 2)
+            load_w1(s, 2)
+        load_w2(3)
 
         pt = ps_o.tile([P, P], BF16, name="pt", tag="ob")
         nc.tensor.transpose(pt[:], b1r[:], ident_b[:])
@@ -117,10 +118,7 @@ def tile_simplefusionmodule_pa_t_kernel(tc, x1, x2, W1, b1, W2, b2, out):
         for i in range(4):
             pb = ps_h.tile([P, 512], F32, name="pb", tag="hb")
             nc.tensor.matmul(pb[:], lhsT=ones_b[:], rhs=b2z[:, i * 512 : (i + 1) * 512], start=True, stop=True)
-            if i % 2 == 0:
-                nc.vector.tensor_copy(out=b2b[:, i * 512 : (i + 1) * 512], in_=pb[:])
-            else:
-                nc.scalar.copy(out=b2b[:, i * 512 : (i + 1) * 512], in_=pb[:])
+            nc.vector.tensor_copy(out=b2b[:, i * 512 : (i + 1) * 512], in_=pb[:])
 
         w2c = const.tile([P, S * F2], U32, name="w2c", align_bytes=64)
         w2s = const.tile([P, S * F2], U8, name="w2s", align_bytes=64)
@@ -136,17 +134,19 @@ def tile_simplefusionmodule_pa_t_kernel(tc, x1, x2, W1, b1, W2, b2, out):
                 in_=src[:, :, c0:c1].rearrange("p t (c i) -> p c t i", i=4),
             )
 
+        def s_cols(s):
+            return W1_S_COLS_FIRST if s == 0 else W1_S_COLS
+
         def w1_src(s):
             h, sl = divmod(s, 2)
             return w1raw[h][:, sl, :, :].rearrange("p u (e c) -> p (u e) c", e=2)
 
         def regroup_w1_s(s):
             w1g[s] = work.tile([P, F1, 4], BF16, name="w1g", tag="w1g", align_bytes=64)
-            if W1_S_COLS > 0:
-                regroup(nc.scalar.copy, w1g[s], w1_src(s), F1 - W1_S_COLS, F1)
+            regroup(nc.scalar.copy, w1g[s], w1_src(s), F1 - s_cols(s), F1)
 
         def regroup_w1_v(s):
-            regroup(nc.vector.tensor_copy, w1g[s], w1_src(s), 0, F1 - W1_S_COLS)
+            regroup(nc.vector.tensor_copy, w1g[s], w1_src(s), 0, F1 - s_cols(s))
 
         def quant_w1(s):
             w1c[s] = work.tile([P, F1], U32, name="w1c", tag="w1c", bufs=3, align_bytes=64)
@@ -156,22 +156,23 @@ def tile_simplefusionmodule_pa_t_kernel(tc, x1, x2, W1, b1, W2, b2, out):
             )
 
         def transposes(s):
-            g, sl = divmod(s, G)
+            sl, n = xt[s][2], xt[s][3]
             xT[s] = []
             for jh in range(2):
                 bank = ps_x.tile([P, 2, 256], F32, name="xT", tag="xT")
                 xT[s].append(bank)
                 for u in range(2):
-                    xf = xt[g][u][:].rearrange("p j s d -> p (j s d)").bitcast(F32)
+                    xf = xt[s][u][:].rearrange("p j s d -> p (j s d)").bitcast(F32)
                     for jl in range(2):
-                        col = ((2 * jh + jl) * G + sl) * P
+                        col = ((2 * jh + jl) * n + sl) * P
                         nc.tensor.transpose(bank[:, u, jl * P : (jl + 1) * P], xf[:, col : col + P], ident_f[:])
 
         def evac_x(s):
             xg[s] = work.tile([P, 4 * B], BF16, name="xg", tag="xg", align_bytes=64)
             xgf = xg[s][:].bitcast(F32).rearrange("p (c u) -> p c u", u=2)
             for jh in range(2):
-                nc.scalar.copy(out=xgf[:, jh * 256 : (jh + 1) * 256, :], in_=xT[s][jh][:].rearrange("p u c -> p c u"))
+                copy = nc.vector.tensor_copy if (s == 0 and jh == 1) else nc.scalar.copy
+                copy(out=xgf[:, jh * 256 : (jh + 1) * 256, :], in_=xT[s][jh][:].rearrange("p u c -> p c u"))
 
         def quant_x(s):
             xc[s] = work.tile([P, B], U32, name="xc", tag="xc", align_bytes=64)
@@ -192,6 +193,72 @@ def tile_simplefusionmodule_pa_t_kernel(tc, x1, x2, W1, b1, W2, b2, out):
                     start=True,
                     stop=True,
                 )
+
+        def layer1_halves(s):
+            hb[s] = []
+            for half in range(2):
+                for tp in range(2):
+                    bank = ps_h.tile([P, 2, 256], F32, name="hb", tag="hb")
+                    hb[s].append(bank)
+                    for e in range(2):
+                        t = 2 * tp + e
+                        nc.tensor.matmul_mx(
+                            out=bank[:, e, :],
+                            lhsT=w1c[s][:, t * P : (t + 1) * P].bitcast(FP8X4),
+                            lhsT_scale=w1s[s][:, t * P : (t + 1) * P],
+                            rhs=xc[s][:, half * 256 : (half + 1) * 256].bitcast(FP8X4),
+                            rhs_scale=xs[s][:, half * 256 : (half + 1) * 256],
+                            start=True,
+                            stop=True,
+                        )
+
+        def evac_h_half(s, half):
+            hp[(s, half)] = work.tile([P, 4, 256], BF16, name="hph", tag="hp")
+            for t in range(4):
+                nc.scalar.activation(
+                    out=hp[(s, half)][:, t, :],
+                    in_=hb[s][2 * half + t // 2][:, t % 2, :],
+                    func=RELU,
+                    bias=b1T[:, 4 * s + t : 4 * s + t + 1],
+                    scale=1.0,
+                )
+
+        def regroup_h_half(s, half):
+            hg[(s, half)] = work.tile([P, 256, 4], BF16, name="hgh", tag="hg", align_bytes=64)
+            regroup(nc.vector.tensor_copy, hg[(s, half)], hp[(s, half)], 0, 256)
+
+        def quant_h_half(s, half):
+            hc[(s, half)] = work.tile([P, 256], U32, name="hch", tag="hc", align_bytes=64)
+            hs[(s, half)] = work.tile([P, 256], U8, name="hsh", tag="hs", align_bytes=64)
+            nc.vector.quantize_mx(
+                out=hc[(s, half)][:].bitcast(FP8X4),
+                scales=hs[(s, half)][:],
+                in_=hg[(s, half)][:].rearrange("p c t -> p (c t)"),
+            )
+
+        def layer2_half(s, half):
+            obh = ps_o.tile([P, 2, F2], F32, name="ob", tag="ob")
+            ob[(s, half)] = obh
+            for jl in range(2):
+                nc.tensor.matmul_mx(
+                    out=obh[:, jl, :],
+                    lhsT=hc[(s, half)][:, jl * P : (jl + 1) * P].bitcast(FP8X4),
+                    lhsT_scale=hs[(s, half)][:, jl * P : (jl + 1) * P],
+                    rhs=w2c[:, s * F2 : (s + 1) * F2].bitcast(FP8X4),
+                    rhs_scale=w2s[:, s * F2 : (s + 1) * F2],
+                    start=True,
+                    stop=True,
+                )
+
+        def evac_o_half(s, half):
+            osh = work.tile([P, 2, F2], F32, name="osh", tag="osb1", bufs=3)
+            nc.vector.tensor_tensor(
+                out=osh[:],
+                in0=ob[(s, half)][:],
+                in1=b2b[:, s * F2 : (s + 1) * F2].unsqueeze(1).to_broadcast([P, 2, F2]),
+                op=ADD,
+            )
+            nc.sync.dma_start(out=outv[:, 2 * half : 2 * half + 2, s, :], in_=osh[:])
 
         def evac_h(s):
             hp[s] = work.tile([P, 4, B], BF16, name="hp", tag="hp")
@@ -237,46 +304,61 @@ def tile_simplefusionmodule_pa_t_kernel(tc, x1, x2, W1, b1, W2, b2, out):
         outv = out.rearrange("(p j) s f -> p j s f", j=4)
 
         def evac_o(s):
-            g, sl = divmod(s, G)
-            if sl == 0:
-                osb[g] = work.tile([P, 4, G, F2], F32, name="osb", tag="osb")
-            nc.vector.tensor_tensor(
-                out=osb[g][:, :, sl, :],
-                in0=ob[s][:],
-                in1=b2b[:, s * F2 : (s + 1) * F2].unsqueeze(1).to_broadcast([P, 4, F2]),
-                op=ADD,
-            )
             for s0, n in STORES:
-                if s0 + n - 1 == s:
-                    nc.sync.dma_start(out=outv[:, :, s0 : s0 + n, :], in_=osb[g][:, :, s0 - g * G : s0 - g * G + n, :])
+                if s0 <= s < s0 + n:
+                    if s == s0:
+                        osb[s0] = work.tile([P, 4, n, F2], F32, name="osb%d" % n, tag="osb%d" % n, bufs=OSB_BUFS[n])
+                    nc.vector.tensor_tensor(
+                        out=osb[s0][:, :, s - s0, :],
+                        in0=ob[s][:],
+                        in1=b2b[:, s * F2 : (s + 1) * F2].unsqueeze(1).to_broadcast([P, 4, F2]),
+                        op=ADD,
+                    )
+                    if s == s0 + n - 1:
+                        nc.sync.dma_start(out=outv[:, :, s0 : s0 + n, :], in_=osb[s0][:])
 
         def on(s):
             return 0 <= s < S
 
-        for k in range(-3, S + 2):
+        for k in range(-2, S):
             if on(k + 2):
                 transposes(k + 2)
-            if on(k - 1):
-                layer2(k - 1)
-            if on(k):
-                evac_h(k)
-            if on(k + 2):
-                regroup_w1_v(k + 2)
             if on(k + 1):
                 quant_x(k + 1)
-                layer1(k + 1)
-            if on(k + 1) and (k + 1) % G == 0:
-                regroup_w2((k + 1) // G)
+            if on(k - 1) and (k - 1) % G == 0:
+                quant_w2((k - 1) // G)
+            if on(k - 1):
+                layer2(k - 1)
+            if on(k) and k != LAST:
+                evac_h(k)
+            if k == LAST:
+                evac_h_half(k, 0)
+                evac_h_half(k, 1)
+            if on(k + 1):
+                quant_w1(k + 1)
+                if k + 1 == LAST:
+                    layer1_halves(k + 1)
+                else:
+                    layer1(k + 1)
             if on(k + 2):
-                quant_w1(k + 2)
                 evac_x(k + 2)
-            if on(k + 3):
-                regroup_w1_s(k + 3)
-            if on(k + 1) and (k + 1) % G == 0:
-                quant_w2((k + 1) // G)
-            if on(k):
+                regroup_w1_s(k + 2)
+            if on(k) and k != LAST:
                 regroup_h(k)
+            if k == LAST:
+                regroup_h_half(k, 0)
+            if on(k + 2):
+                regroup_w1_v(k + 2)
             if on(k - 1):
                 evac_o(k - 1)
-            if on(k):
+            if on(k) and k != LAST:
                 quant_h(k)
+            if on(k) and k % G == 0:
+                regroup_w2(k // G)
+        quant_h_half(LAST, 0)
+        layer2_half(LAST, 0)
+        regroup_h_half(LAST, 1)
+        quant_h_half(LAST, 1)
+        layer2_half(LAST, 1)
+        evac_o_half(LAST, 0)
+        evac_o_half(LAST, 1)

@@ -20,8 +20,9 @@ K = 2 * D
 FLOPS = 2 * S * B * K * F1 + 2 * S * B * F1 * F2
 
 MANUAL = True
-W1_S_COLS = 256
-W1_S_COLS_FIRST = 128
+W1_S_COLS = 240
+W1_S_COLS_HEAD = {0: 0, 1: 0}
+RH_S_COLS = {13: 64, 14: 128}
 LAST = 15
 OSB_BUFS = {4: 2, 2: 1, 1: 3}
 G = 4
@@ -87,7 +88,9 @@ def tile_simplefusionmodule_pa_t_kernel(tc, x1, x2, W1, b1, W2, b2, out):
 
         alloc_w1(0)
         alloc_w1(1)
-        for s in range(3):
+        load_w1(0, 1)
+        load_x_styles(0, 1)
+        for s in (1, 2):
             load_x_styles(s, 1)
             load_w1(s, 1)
         load_w2(0)
@@ -118,7 +121,7 @@ def tile_simplefusionmodule_pa_t_kernel(tc, x1, x2, W1, b1, W2, b2, out):
         for i in range(4):
             pb = ps_h.tile([P, 512], F32, name="pb", tag="hb")
             nc.tensor.matmul(pb[:], lhsT=ones_b[:], rhs=b2z[:, i * 512 : (i + 1) * 512], start=True, stop=True)
-            nc.vector.tensor_copy(out=b2b[:, i * 512 : (i + 1) * 512], in_=pb[:])
+            nc.scalar.copy(out=b2b[:, i * 512 : (i + 1) * 512], in_=pb[:])
 
         w2c = const.tile([P, S * F2], U32, name="w2c", align_bytes=64)
         w2s = const.tile([P, S * F2], U8, name="w2s", align_bytes=64)
@@ -135,7 +138,7 @@ def tile_simplefusionmodule_pa_t_kernel(tc, x1, x2, W1, b1, W2, b2, out):
             )
 
         def s_cols(s):
-            return W1_S_COLS_FIRST if s == 0 else W1_S_COLS
+            return W1_S_COLS_HEAD.get(s, W1_S_COLS)
 
         def w1_src(s):
             h, sl = divmod(s, 2)
@@ -143,7 +146,8 @@ def tile_simplefusionmodule_pa_t_kernel(tc, x1, x2, W1, b1, W2, b2, out):
 
         def regroup_w1_s(s):
             w1g[s] = work.tile([P, F1, 4], BF16, name="w1g", tag="w1g", align_bytes=64)
-            regroup(nc.scalar.copy, w1g[s], w1_src(s), F1 - s_cols(s), F1)
+            if s_cols(s) > 0:
+                regroup(nc.scalar.copy, w1g[s], w1_src(s), F1 - s_cols(s), F1)
 
         def regroup_w1_v(s):
             regroup(nc.vector.tensor_copy, w1g[s], w1_src(s), 0, F1 - s_cols(s))
@@ -269,7 +273,10 @@ def tile_simplefusionmodule_pa_t_kernel(tc, x1, x2, W1, b1, W2, b2, out):
 
         def regroup_h(s):
             hg[s] = work.tile([P, B, 4], BF16, name="hg", tag="hg", align_bytes=64)
-            regroup(nc.vector.tensor_copy, hg[s], hp[s], 0, B)
+            n = RH_S_COLS.get(s, 0)
+            if n > 0:
+                regroup(nc.scalar.copy, hg[s], hp[s], B - n, B)
+            regroup(nc.vector.tensor_copy, hg[s], hp[s], 0, B - n)
 
         def quant_h(s):
             hc[s] = work.tile([P, B], U32, name="hc", tag="hc", align_bytes=64)
@@ -320,7 +327,18 @@ def tile_simplefusionmodule_pa_t_kernel(tc, x1, x2, W1, b1, W2, b2, out):
         def on(s):
             return 0 <= s < S
 
-        for k in range(-2, S):
+        regroup_w1_s(0)
+        regroup_w1_v(0)
+        quant_w1(0)
+        transposes(0)
+        evac_x(0)
+        transposes(1)
+        quant_x(0)
+        layer1(0)
+        evac_x(1)
+        regroup_w1_s(1)
+        regroup_w1_v(1)
+        for k in range(0, S):
             if on(k + 2):
                 transposes(k + 2)
             if on(k + 1):

@@ -20,7 +20,7 @@ K = 2 * D
 FLOPS = 2 * S * B * K * F1 + 2 * S * B * F1 * F2
 
 MANUAL = True
-W1_S_COLS = 240
+W1_S_COLS = 176
 W1_S_COLS_HEAD = {0: 0, 1: 0}
 RH_S_COLS = {13: 64, 14: 128}
 LAST = 15

@@ -20,11 +20,11 @@ K = 2 * D
 FLOPS = 2 * S * B * K * F1 + 2 * S * B * F1 * F2
 
 MANUAL = True
-W1_S_COLS = 176
+W1_S_COLS = 240
 W1_S_COLS_HEAD = {0: 0, 1: 0}
 RH_S_COLS = {13: 64, 14: 128}
 LAST = 15
-OSB_BUFS = {4: 2, 2: 1, 1: 3}
+OSB_BUFS = {4: 3, 2: 1, 1: 3}
 G = 4
 STORES = ((0, 4), (4, 4), (8, 4), (12, 2), (14, 1))
 

@@ -19,9 +19,9 @@ B, S, D, F1, F2 = 512, 16, 256, 512, 128
 K = 2 * D
 FLOPS = 2 * S * B * K * F1 + 2 * S * B * F1 * F2
 
-MANUAL = True
-W1_S_COLS = 240
-W1_S_COLS_HEAD = {0: 0, 1: 0}
+W1_S_COLS = {2: 240}
+W1_PE_COLS = 256
+W1_PE_FIRST = 3
 RH_S_COLS = {13: 64, 14: 128}
 LAST = 15
 OSB_BUFS = {4: 3, 2: 1, 1: 3}
@@ -38,22 +38,16 @@ def tile_simplefusionmodule_pa_t_kernel(tc, x1, x2, W1, b1, W2, b2, out):
         work = ctx.enter_context(tc.tile_pool(name="work", bufs=2))
         ps_x = ctx.enter_context(tc.psum_pool(name="ps_x", bufs=2))
         ps_h = ctx.enter_context(tc.psum_pool(name="ps_h", bufs=4))
-        ps_o = ctx.enter_context(tc.psum_pool(name="ps_o", bufs=2))
-        if MANUAL:
-            ctx.enter_context(tc.manual_schedule())
+        ps_o = ctx.enter_context(tc.psum_pool(name="ps_o", bufs=1))
+        ps_w = ctx.enter_context(tc.psum_pool(name="ps_w", bufs=1))
+        ctx.enter_context(tc.manual_schedule())
 
-        b1r = const.tile([P, P], BF16, name="b1r")
-        nc.vector.memset(b1r[:].bitcast(I32), 0)
-        nc.sync.dma_start(out=b1r[0:64, :], in_=b1.rearrange("s (t p) -> (s t) p", p=P))
-        b2z = const.tile([P, S * F2], BF16, name="b2z")
-        nc.vector.memset(b2z[:].bitcast(I32), 0)
-        nc.sync.dma_start(out=b2z[0:1, :], in_=b2.rearrange("(o s) f -> o (s f)", o=1))
+        br = const.tile([P, P], BF16, name="br")
+        nc.vector.memset(br[:].bitcast(I32), 0)
         ident_f = const.tile([P, P], F32, name="ident_f")
         make_identity(nc, ident_f[:])
         ident_b = const.tile([P, P], BF16, name="ident_b")
         make_identity(nc, ident_b[:])
-        ones_b = const.tile([P, P], BF16, name="ones_b")
-        nc.gpsimd.memset(ones_b[:], 1.0)
 
         x1v = x1.rearrange("(p j) s d -> p j s d", j=4)
         x2v = x2.rearrange("(p j) s d -> p j s d", j=4)
@@ -89,6 +83,8 @@ def tile_simplefusionmodule_pa_t_kernel(tc, x1, x2, W1, b1, W2, b2, out):
         alloc_w1(0)
         alloc_w1(1)
         load_w1(0, 1)
+        nc.sync.dma_start(out=br[0:64, :], in_=b1.rearrange("s (t p) -> (s t) p", p=P))
+        nc.sync.dma_start(out=br[64:80, :], in_=b2[:, :])
         load_x_styles(0, 1)
         for s in (1, 2):
             load_x_styles(s, 1)
@@ -114,20 +110,27 @@ def tile_simplefusionmodule_pa_t_kernel(tc, x1, x2, W1, b1, W2, b2, out):
         load_w2(3)
 
         pt = ps_o.tile([P, P], BF16, name="pt", tag="ob")
-        nc.tensor.transpose(pt[:], b1r[:], ident_b[:])
+        nc.tensor.transpose(pt[:], br[:], ident_b[:])
         b1T = const.tile([P, 64], F32, name="b1T")
-        nc.vector.tensor_copy(out=b1T[:], in_=pt[:, 0:64])
         b2b = const.tile([P, S * F2], F32, name="b2b")
-        for i in range(4):
+        def spread_b2(i):
             pb = ps_h.tile([P, 512], F32, name="pb", tag="hb")
-            nc.tensor.matmul(pb[:], lhsT=ones_b[:], rhs=b2z[:, i * 512 : (i + 1) * 512], start=True, stop=True)
+            for j in range(4):
+                row = 64 + 4 * i + j
+                nc.tensor.matmul(
+                    pb[:, j * F2 : (j + 1) * F2],
+                    lhsT=ident_b[:, row : row + 1].to_broadcast([P, P]),
+                    rhs=br[:],
+                    start=True,
+                    stop=True,
+                )
             nc.scalar.copy(out=b2b[:, i * 512 : (i + 1) * 512], in_=pb[:])
 
         w2c = const.tile([P, S * F2], U32, name="w2c", align_bytes=64)
         w2s = const.tile([P, S * F2], U8, name="w2s", align_bytes=64)
 
         xT, xg, xc, xs = {}, {}, {}, {}
-        w1g, w1c, w1s = {}, {}, {}
+        w1g, w1c, w1s, wb = {}, {}, {}, {}
         hb, hp, hg, hc, hs = {}, {}, {}, {}, {}
         ob, osb, w2g = {}, {}, {}
 
@@ -138,19 +141,39 @@ def tile_simplefusionmodule_pa_t_kernel(tc, x1, x2, W1, b1, W2, b2, out):
             )
 
         def s_cols(s):
-            return W1_S_COLS_HEAD.get(s, W1_S_COLS)
+            return W1_S_COLS.get(s, 0)
+
+        def pe_cols(s):
+            return W1_PE_COLS if s >= W1_PE_FIRST else 0
 
         def w1_src(s):
             h, sl = divmod(s, 2)
             return w1raw[h][:, sl, :, :].rearrange("p u (e c) -> p (u e) c", e=2)
 
+        def regroup_w1_pe(s):
+            n = pe_cols(s)
+            if n > 0:
+                wb[s] = ps_w.tile([P, 4 * n], BF16, name="wb", tag="wb")
+                for i in range(n // P):
+                    c0 = F1 - n + i * P
+                    nc.tensor.matmul(
+                        wb[s][:, i * 512 : (i + 1) * 512],
+                        lhsT=ident_b[:],
+                        rhs=w1_src(s)[:, :, c0 : c0 + P].rearrange("p t c -> p c t"),
+                        start=True,
+                        stop=True,
+                    )
+
         def regroup_w1_s(s):
             w1g[s] = work.tile([P, F1, 4], BF16, name="w1g", tag="w1g", align_bytes=64)
+            n = pe_cols(s)
+            if n > 0:
+                nc.scalar.copy(out=w1g[s][:, F1 - n : F1, :].rearrange("p c t -> p (c t)"), in_=wb[s][:])
             if s_cols(s) > 0:
                 regroup(nc.scalar.copy, w1g[s], w1_src(s), F1 - s_cols(s), F1)
 
         def regroup_w1_v(s):
-            regroup(nc.vector.tensor_copy, w1g[s], w1_src(s), 0, F1 - s_cols(s))
+            regroup(nc.vector.tensor_copy, w1g[s], w1_src(s), 0, F1 - s_cols(s) - pe_cols(s))
 
         def quant_w1(s):
             w1c[s] = work.tile([P, F1], U32, name="w1c", tag="w1c", bufs=3, align_bytes=64)
@@ -241,7 +264,7 @@ def tile_simplefusionmodule_pa_t_kernel(tc, x1, x2, W1, b1, W2, b2, out):
             )
 
         def layer2_half(s, half):
-            obh = ps_o.tile([P, 2, F2], F32, name="ob", tag="ob")
+            obh = ps_x.tile([P, 2, F2], F32, name="obh", tag="xT")
             ob[(s, half)] = obh
             for jl in range(2):
                 nc.tensor.matmul_mx(
@@ -327,11 +350,16 @@ def tile_simplefusionmodule_pa_t_kernel(tc, x1, x2, W1, b1, W2, b2, out):
         def on(s):
             return 0 <= s < S
 
+        spread_b2(0)
+        spread_b2(1)
         regroup_w1_s(0)
         regroup_w1_v(0)
+        nc.vector.tensor_copy(out=b1T[:], in_=pt[:, 0:64])
         quant_w1(0)
         transposes(0)
         evac_x(0)
+        spread_b2(2)
+        spread_b2(3)
         transposes(1)
         quant_x(0)
         layer1(0)
@@ -341,6 +369,7 @@ def tile_simplefusionmodule_pa_t_kernel(tc, x1, x2, W1, b1, W2, b2, out):
         for k in range(0, S):
             if on(k + 2):
                 transposes(k + 2)
+                regroup_w1_pe(k + 2)
             if on(k + 1):
                 quant_x(k + 1)
             if on(k - 1) and (k - 1) % G == 0:

@@ -23,6 +23,7 @@ W1_S_COLS = {2: 240}
 W1_PE_COLS = 256
 W1_PE_FIRST = 3
 RH_S_COLS = {13: 64, 14: 128}
+RUN = 8
 LAST = 15
 OSB_BUFS = {4: 3, 2: 1, 1: 3}
 G = 4
@@ -136,8 +137,8 @@ def tile_simplefusionmodule_pa_t_kernel(tc, x1, x2, W1, b1, W2, b2, out):
 
         def regroup(eng_copy, dst, src, c0, c1):
             eng_copy(
-                out=dst[:, c0:c1, :].rearrange("p (c i) t -> p c t i", i=4),
-                in_=src[:, :, c0:c1].rearrange("p t (c i) -> p c t i", i=4),
+                out=dst[:, c0:c1, :].rearrange("p (c i) t -> p c t i", i=RUN),
+                in_=src[:, :, c0:c1].rearrange("p t (c i) -> p c t i", i=RUN),
             )
 
         def s_cols(s):

@@ -19,7 +19,8 @@ B, S, D, F1, F2 = 512, 16, 256, 512, 128
 K = 2 * D
 FLOPS = 2 * S * B * K * F1 + 2 * S * B * F1 * F2
 
-W1_S_COLS = {2: 240}
+W1_S_COLS = 96
+W1_S_COLS_HEAD = {0: 0, 1: 0, 2: 240}
 W1_PE_COLS = 256
 W1_PE_FIRST = 3
 RH_S_COLS = {13: 64, 14: 128}
@@ -142,7 +143,7 @@ def tile_simplefusionmodule_pa_t_kernel(tc, x1, x2, W1, b1, W2, b2, out):
             )
 
         def s_cols(s):
-            return W1_S_COLS.get(s, 0)
+            return W1_S_COLS_HEAD.get(s, W1_S_COLS)
 
         def pe_cols(s):
             return W1_PE_COLS if s >= W1_PE_FIRST else 0
@@ -171,7 +172,7 @@ def tile_simplefusionmodule_pa_t_kernel(tc, x1, x2, W1, b1, W2, b2, out):
             if n > 0:
                 nc.scalar.copy(out=w1g[s][:, F1 - n : F1, :].rearrange("p c t -> p (c t)"), in_=wb[s][:])
             if s_cols(s) > 0:
-                regroup(nc.scalar.copy, w1g[s], w1_src(s), F1 - s_cols(s), F1)
+                regroup(nc.scalar.copy, w1g[s], w1_src(s), F1 - n - s_cols(s), F1 - n)
 
         def regroup_w1_v(s):
             regroup(nc.vector.tensor_copy, w1g[s], w1_src(s), 0, F1 - s_cols(s) - pe_cols(s))

@@ -19,7 +19,7 @@ B, S, D, F1, F2 = 512, 16, 256, 512, 128
 K = 2 * D
 FLOPS = 2 * S * B * K * F1 + 2 * S * B * F1 * F2
 
-W1_S_COLS = 96
+W1_S_COLS = 48
 W1_S_COLS_HEAD = {0: 0, 1: 0, 2: 240}
 W1_PE_COLS = 256
 W1_PE_FIRST = 3
@@ -132,6 +132,7 @@ def tile_simplefusionmodule_pa_t_kernel(tc, x1, x2, W1, b1, W2, b2, out):
         w2s = const.tile([P, S * F2], U8, name="w2s", align_bytes=64)
 
         xT, xg, xc, xs = {}, {}, {}, {}
+        xwg, xwc, xws = {}, {}, {}
         w1g, w1c, w1s, wb = {}, {}, {}, {}
         hb, hp, hg, hc, hs = {}, {}, {}, {}, {}
         ob, osb, w2g = {}, {}, {}
@@ -166,8 +167,22 @@ def tile_simplefusionmodule_pa_t_kernel(tc, x1, x2, W1, b1, W2, b2, out):
                         stop=True,
                     )
 
+        def alloc_xw(s):
+            xwg[s] = work.tile([P, B + F1, 4], BF16, name="xwg", tag="xwg", align_bytes=64)
+            xwc[s] = work.tile([P, B + F1], U32, name="xwc", tag="xwc", bufs=3, align_bytes=64)
+            xws[s] = work.tile([P, B + F1], U8, name="xws", tag="xws", bufs=3, align_bytes=64)
+            xg[s], w1g[s] = xwg[s][:, 0:B, :], xwg[s][:, B : B + F1, :]
+            xc[s], w1c[s] = xwc[s][:, 0:B], xwc[s][:, B : B + F1]
+            xs[s], w1s[s] = xws[s][:, 0:B], xws[s][:, B : B + F1]
+
+        def quant_xw(s, c0, c1):
+            nc.vector.quantize_mx(
+                out=xwc[s][:, c0:c1].bitcast(FP8X4),
+                scales=xws[s][:, c0:c1],
+                in_=xwg[s][:, c0:c1, :].rearrange("p c t -> p (c t)"),
+            )
+
         def regroup_w1_s(s):
-            w1g[s] = work.tile([P, F1, 4], BF16, name="w1g", tag="w1g", align_bytes=64)
             n = pe_cols(s)
             if n > 0:
                 nc.scalar.copy(out=w1g[s][:, F1 - n : F1, :].rearrange("p c t -> p (c t)"), in_=wb[s][:])
@@ -176,13 +191,6 @@ def tile_simplefusionmodule_pa_t_kernel(tc, x1, x2, W1, b1, W2, b2, out):
 
         def regroup_w1_v(s):
             regroup(nc.vector.tensor_copy, w1g[s], w1_src(s), 0, F1 - s_cols(s) - pe_cols(s))
-
-        def quant_w1(s):
-            w1c[s] = work.tile([P, F1], U32, name="w1c", tag="w1c", bufs=3, align_bytes=64)
-            w1s[s] = work.tile([P, F1], U8, name="w1s", tag="w1s", bufs=3, align_bytes=64)
-            nc.vector.quantize_mx(
-                out=w1c[s][:].bitcast(FP8X4), scales=w1s[s][:], in_=w1g[s][:].rearrange("p c t -> p (c t)")
-            )
 
         def transposes(s):
             sl, n = xt[s][2], xt[s][3]
@@ -197,16 +205,10 @@ def tile_simplefusionmodule_pa_t_kernel(tc, x1, x2, W1, b1, W2, b2, out):
                         nc.tensor.transpose(bank[:, u, jl * P : (jl + 1) * P], xf[:, col : col + P], ident_f[:])
 
         def evac_x(s):
-            xg[s] = work.tile([P, 4 * B], BF16, name="xg", tag="xg", align_bytes=64)
-            xgf = xg[s][:].bitcast(F32).rearrange("p (c u) -> p c u", u=2)
+            xgf = xg[s].rearrange("p c t -> p (c t)").bitcast(F32).rearrange("p (c u) -> p c u", u=2)
             for jh in range(2):
                 copy = nc.vector.tensor_copy if (s == 0 and jh == 1) else nc.scalar.copy
                 copy(out=xgf[:, jh * 256 : (jh + 1) * 256, :], in_=xT[s][jh][:].rearrange("p u c -> p c u"))
-
-        def quant_x(s):
-            xc[s] = work.tile([P, B], U32, name="xc", tag="xc", align_bytes=64)
-            xs[s] = work.tile([P, B], U8, name="xs", tag="xs", align_bytes=64)
-            nc.vector.quantize_mx(out=xc[s][:].bitcast(FP8X4), scales=xs[s][:], in_=xg[s][:])
 
         def layer1(s):
             hb[s] = []
@@ -217,8 +219,8 @@ def tile_simplefusionmodule_pa_t_kernel(tc, x1, x2, W1, b1, W2, b2, out):
                     out=bank[:],
                     lhsT=w1c[s][:, t * P : (t + 1) * P].bitcast(FP8X4),
                     lhsT_scale=w1s[s][:, t * P : (t + 1) * P],
-                    rhs=xc[s][:].bitcast(FP8X4),
-                    rhs_scale=xs[s][:],
+                    rhs=xc[s].bitcast(FP8X4),
+                    rhs_scale=xs[s],
                     start=True,
                     stop=True,
                 )
@@ -354,17 +356,19 @@ def tile_simplefusionmodule_pa_t_kernel(tc, x1, x2, W1, b1, W2, b2, out):
 
         spread_b2(0)
         spread_b2(1)
+        alloc_xw(0)
         regroup_w1_s(0)
         regroup_w1_v(0)
         nc.vector.tensor_copy(out=b1T[:], in_=pt[:, 0:64])
-        quant_w1(0)
+        quant_xw(0, B, B + F1)
         transposes(0)
         evac_x(0)
         spread_b2(2)
         spread_b2(3)
         transposes(1)
-        quant_x(0)
+        quant_xw(0, 0, B)
         layer1(0)
+        alloc_xw(1)
         evac_x(1)
         regroup_w1_s(1)
         regroup_w1_v(1)
@@ -373,7 +377,7 @@ def tile_simplefusionmodule_pa_t_kernel(tc, x1, x2, W1, b1, W2, b2, out):
                 transposes(k + 2)
                 regroup_w1_pe(k + 2)
             if on(k + 1):
-                quant_x(k + 1)
+                quant_xw(k + 1, 0, B + F1)
             if on(k - 1) and (k - 1) % G == 0:
                 quant_w2((k - 1) // G)
             if on(k - 1):
@@ -384,20 +388,20 @@ def tile_simplefusionmodule_pa_t_kernel(tc, x1, x2, W1, b1, W2, b2, out):
                 evac_h_half(k, 0)
                 evac_h_half(k, 1)
             if on(k + 1):
-                quant_w1(k + 1)
                 if k + 1 == LAST:
                     layer1_halves(k + 1)
                 else:
                     layer1(k + 1)
             if on(k + 2):
+                alloc_xw(k + 2)
                 evac_x(k + 2)
                 regroup_w1_s(k + 2)
+            if on(k + 2):
+                regroup_w1_v(k + 2)
             if on(k) and k != LAST:
                 regroup_h(k)
             if k == LAST:
                 regroup_h_half(k, 0)
-            if on(k + 2):
-                regroup_w1_v(k + 2)
             if on(k - 1):
                 evac_o(k - 1)
             if on(k) and k != LAST:

@@ -19,12 +19,13 @@ B, S, D, F1, F2 = 512, 16, 256, 512, 128
 K = 2 * D
 FLOPS = 2 * S * B * K * F1 + 2 * S * B * F1 * F2
 
-W1_S_COLS = 48
+W1_S_COLS = 72
 W1_S_COLS_HEAD = {0: 0, 1: 0, 2: 240}
 W1_PE_COLS = 256
 W1_PE_FIRST = 3
 RH_S_COLS = {13: 64, 14: 128}
 RUN = 8
+RH_S_COLS_END = (0, 80)
 LAST = 15
 OSB_BUFS = {4: 3, 2: 1, 1: 3}
 G = 4
@@ -88,9 +89,10 @@ def tile_simplefusionmodule_pa_t_kernel(tc, x1, x2, W1, b1, W2, b2, out):
         nc.sync.dma_start(out=br[0:64, :], in_=b1.rearrange("s (t p) -> (s t) p", p=P))
         nc.sync.dma_start(out=br[64:80, :], in_=b2[:, :])
         load_x_styles(0, 1)
-        for s in (1, 2):
-            load_x_styles(s, 1)
-            load_w1(s, 1)
+        load_w1(1, 1)
+        load_x_styles(1, 1)
+        load_x_styles(2, 1)
+        load_w1(2, 1)
         load_w2(0)
         load_x_styles(3, 1)
         load_w1(3, 1)
@@ -115,7 +117,7 @@ def tile_simplefusionmodule_pa_t_kernel(tc, x1, x2, W1, b1, W2, b2, out):
         nc.tensor.transpose(pt[:], br[:], ident_b[:])
         b1T = const.tile([P, 64], F32, name="b1T")
         b2b = const.tile([P, S * F2], F32, name="b2b")
-        def spread_b2(i):
+        def spread_b2(i, copy):
             pb = ps_h.tile([P, 512], F32, name="pb", tag="hb")
             for j in range(4):
                 row = 64 + 4 * i + j
@@ -126,7 +128,7 @@ def tile_simplefusionmodule_pa_t_kernel(tc, x1, x2, W1, b1, W2, b2, out):
                     start=True,
                     stop=True,
                 )
-            nc.scalar.copy(out=b2b[:, i * 512 : (i + 1) * 512], in_=pb[:])
+            copy(out=b2b[:, i * 512 : (i + 1) * 512], in_=pb[:])
 
         w2c = const.tile([P, S * F2], U32, name="w2c", align_bytes=64)
         w2s = const.tile([P, S * F2], U8, name="w2s", align_bytes=64)
@@ -185,7 +187,9 @@ def tile_simplefusionmodule_pa_t_kernel(tc, x1, x2, W1, b1, W2, b2, out):
         def regroup_w1_s(s):
             n = pe_cols(s)
             if n > 0:
-                nc.scalar.copy(out=w1g[s][:, F1 - n : F1, :].rearrange("p c t -> p (c t)"), in_=wb[s][:])
+                nc.scalar.copy(
+                    out=w1g[s][:, F1 - n : F1, :].rearrange("p c t -> p (c t)").bitcast(F32), in_=wb[s][:].bitcast(F32)
+                )
             if s_cols(s) > 0:
                 regroup(nc.scalar.copy, w1g[s], w1_src(s), F1 - n - s_cols(s), F1 - n)
 
@@ -207,8 +211,7 @@ def tile_simplefusionmodule_pa_t_kernel(tc, x1, x2, W1, b1, W2, b2, out):
         def evac_x(s):
             xgf = xg[s].rearrange("p c t -> p (c t)").bitcast(F32).rearrange("p (c u) -> p c u", u=2)
             for jh in range(2):
-                copy = nc.vector.tensor_copy if (s == 0 and jh == 1) else nc.scalar.copy
-                copy(out=xgf[:, jh * 256 : (jh + 1) * 256, :], in_=xT[s][jh][:].rearrange("p u c -> p c u"))
+                nc.scalar.copy(out=xgf[:, jh * 256 : (jh + 1) * 256, :], in_=xT[s][jh][:].rearrange("p u c -> p c u"))
 
         def layer1(s):
             hb[s] = []
@@ -256,7 +259,10 @@ def tile_simplefusionmodule_pa_t_kernel(tc, x1, x2, W1, b1, W2, b2, out):
 
         def regroup_h_half(s, half):
             hg[(s, half)] = work.tile([P, 256, 4], BF16, name="hgh", tag="hg", align_bytes=64)
-            regroup(nc.vector.tensor_copy, hg[(s, half)], hp[(s, half)], 0, 256)
+            n = RH_S_COLS_END[half]
+            if n > 0:
+                regroup(nc.scalar.copy, hg[(s, half)], hp[(s, half)], 256 - n, 256)
+            regroup(nc.vector.tensor_copy, hg[(s, half)], hp[(s, half)], 0, 256 - n)
 
         def quant_h_half(s, half):
             hc[(s, half)] = work.tile([P, 256], U32, name="hch", tag="hc", align_bytes=64)
@@ -354,8 +360,8 @@ def tile_simplefusionmodule_pa_t_kernel(tc, x1, x2, W1, b1, W2, b2, out):
         def on(s):
             return 0 <= s < S
 
-        spread_b2(0)
-        spread_b2(1)
+        spread_b2(0, nc.scalar.copy)
+        spread_b2(1, nc.scalar.copy)
         alloc_xw(0)
         regroup_w1_s(0)
         regroup_w1_v(0)
@@ -363,15 +369,15 @@ def tile_simplefusionmodule_pa_t_kernel(tc, x1, x2, W1, b1, W2, b2, out):
         quant_xw(0, B, B + F1)
         transposes(0)
         evac_x(0)
-        spread_b2(2)
-        spread_b2(3)
         transposes(1)
-        quant_xw(0, 0, B)
-        layer1(0)
         alloc_xw(1)
-        evac_x(1)
         regroup_w1_s(1)
         regroup_w1_v(1)
+        quant_xw(0, 0, B)
+        spread_b2(2, nc.vector.tensor_copy)
+        spread_b2(3, nc.vector.tensor_copy)
+        layer1(0)
+        evac_x(1)
         for k in range(0, S):
             if on(k + 2):
                 transposes(k + 2)

@@ -19,11 +19,11 @@ B, S, D, F1, F2 = 512, 16, 256, 512, 128
 K = 2 * D
 FLOPS = 2 * S * B * K * F1 + 2 * S * B * F1 * F2
 
-W1_S_COLS = 72
+W1_S_COLS = 56
 W1_S_COLS_HEAD = {0: 0, 1: 0, 2: 240}
 W1_PE_COLS = 256
 W1_PE_FIRST = 3
-RH_S_COLS = {13: 64, 14: 128}
+RH_S_COLS = {13: 64, 14: 192}
 RUN = 8
 RH_S_COLS_END = (0, 80)
 LAST = 15
@@ -89,10 +89,9 @@ def tile_simplefusionmodule_pa_t_kernel(tc, x1, x2, W1, b1, W2, b2, out):
         nc.sync.dma_start(out=br[0:64, :], in_=b1.rearrange("s (t p) -> (s t) p", p=P))
         nc.sync.dma_start(out=br[64:80, :], in_=b2[:, :])
         load_x_styles(0, 1)
-        load_w1(1, 1)
-        load_x_styles(1, 1)
-        load_x_styles(2, 1)
-        load_w1(2, 1)
+        for s in (1, 2):
+            load_x_styles(s, 1)
+            load_w1(s, 1)
         load_w2(0)
         load_x_styles(3, 1)
         load_w1(3, 1)
@@ -159,12 +158,11 @@ def tile_simplefusionmodule_pa_t_kernel(tc, x1, x2, W1, b1, W2, b2, out):
             n = pe_cols(s)
             if n > 0:
                 wb[s] = ps_w.tile([P, 4 * n], BF16, name="wb", tag="wb")
-                for i in range(n // P):
-                    c0 = F1 - n + i * P
+                for t in (0, 2):
                     nc.tensor.matmul(
-                        wb[s][:, i * 512 : (i + 1) * 512],
+                        wb[s][:].rearrange("p (c t) -> p c t", t=4)[:, :, t : t + 2],
                         lhsT=ident_b[:],
-                        rhs=w1_src(s)[:, :, c0 : c0 + P].rearrange("p t c -> p c t"),
+                        rhs=w1_src(s)[:, t : t + 2, F1 - n : F1].rearrange("p t c -> p c t"),
                         start=True,
                         stop=True,
                     )
@@ -211,7 +209,8 @@ def tile_simplefusionmodule_pa_t_kernel(tc, x1, x2, W1, b1, W2, b2, out):
         def evac_x(s):
             xgf = xg[s].rearrange("p c t -> p (c t)").bitcast(F32).rearrange("p (c u) -> p c u", u=2)
             for jh in range(2):
-                nc.scalar.copy(out=xgf[:, jh * 256 : (jh + 1) * 256, :], in_=xT[s][jh][:].rearrange("p u c -> p c u"))
+                copy = nc.vector.tensor_copy if (s == 0 and jh == 1) else nc.scalar.copy
+                copy(out=xgf[:, jh * 256 : (jh + 1) * 256, :], in_=xT[s][jh][:].rearrange("p u c -> p c u"))
 
         def layer1(s):
             hb[s] = []
@@ -362,6 +361,7 @@ def tile_simplefusionmodule_pa_t_kernel(tc, x1, x2, W1, b1, W2, b2, out):
 
         spread_b2(0, nc.scalar.copy)
         spread_b2(1, nc.scalar.copy)
+        spread_b2(3, nc.scalar.copy)
         alloc_xw(0)
         regroup_w1_s(0)
         regroup_w1_v(0)
@@ -369,15 +369,14 @@ def tile_simplefusionmodule_pa_t_kernel(tc, x1, x2, W1, b1, W2, b2, out):
         quant_xw(0, B, B + F1)
         transposes(0)
         evac_x(0)
+        spread_b2(2, nc.vector.tensor_copy)
+        quant_xw(0, 0, B)
         transposes(1)
+        layer1(0)
         alloc_xw(1)
+        evac_x(1)
         regroup_w1_s(1)
         regroup_w1_v(1)
-        quant_xw(0, 0, B)
-        spread_b2(2, nc.vector.tensor_copy)
-        spread_b2(3, nc.vector.tensor_copy)
-        layer1(0)
-        evac_x(1)
         for k in range(0, S):
             if on(k + 2):
                 transposes(k + 2)

@@ -23,6 +23,7 @@ W1_S_COLS = 56
 W1_S_COLS_HEAD = {0: 0, 1: 0, 2: 240}
 W1_PE_COLS = 256
 W1_PE_FIRST = 3
+W2_S_COLS = 128
 RH_S_COLS = {13: 64, 14: 192}
 RUN = 8
 RH_S_COLS_END = (0, 80)
@@ -319,7 +320,8 @@ def tile_simplefusionmodule_pa_t_kernel(tc, x1, x2, W1, b1, W2, b2, out):
 
         def regroup_w2(q):
             w2g[q] = work.tile([P, G * F2, 4], BF16, name="w2g", tag="w2g", bufs=1, align_bytes=64)
-            regroup(nc.vector.tensor_copy, w2g[q], w2raw[:, q, :, :], 0, G * F2)
+            regroup(nc.scalar.copy, w2g[q], w2raw[:, q, :, :], G * F2 - W2_S_COLS, G * F2)
+            regroup(nc.vector.tensor_copy, w2g[q], w2raw[:, q, :, :], 0, G * F2 - W2_S_COLS)
 
         def quant_w2(q):
             cols = slice(q * G * F2, (q + 1) * G * F2)

from contextlib import ExitStack

import concourse.bass as bass
import concourse.mybir as mybir
import concourse.tile as tile
from concourse.masks import make_identity

F32 = mybir.dt.float32
BF16 = mybir.dt.bfloat16
I32 = mybir.dt.int32
U32 = mybir.dt.uint32
U8 = mybir.dt.uint8
FP8X4 = mybir.dt.float8_e4m3fn_x4
RELU = mybir.ActivationFunctionType.Relu
ADD = mybir.AluOpType.add

P = 128
B, S, D, F1, F2 = 512, 16, 256, 512, 128
K = 2 * D
FLOPS = 2 * S * B * K * F1 + 2 * S * B * F1 * F2

W1_S_COLS = 56
W1_S_COLS_HEAD = {0: 0, 1: 0, 2: 240}
W1_PE_COLS = 256
W1_PE_FIRST = 3
W2_S_COLS = 128
RH_S_COLS = {13: 64, 14: 192}
RUN = 8
RH_S_COLS_END = (0, 80)
LAST = 15
OSB_BUFS = {4: 3, 2: 1, 1: 3}
G = 4
STORES = ((0, 4), (4, 4), (8, 4), (12, 2), (14, 1))


def tile_simplefusionmodule_pa_t_kernel(tc, x1, x2, W1, b1, W2, b2, out):
    nc = tc.nc
    with ExitStack() as ctx:
        const = ctx.enter_context(tc.tile_pool(name="const", bufs=1))
        xpool = ctx.enter_context(tc.tile_pool(name="xpool", bufs=1))
        w1pool = ctx.enter_context(tc.tile_pool(name="w1pool", bufs=5))
        work = ctx.enter_context(tc.tile_pool(name="work", bufs=2))
        ps_x = ctx.enter_context(tc.psum_pool(name="ps_x", bufs=2))
        ps_h = ctx.enter_context(tc.psum_pool(name="ps_h", bufs=4))
        ps_o = ctx.enter_context(tc.psum_pool(name="ps_o", bufs=1))
        ps_w = ctx.enter_context(tc.psum_pool(name="ps_w", bufs=1))
        ctx.enter_context(tc.manual_schedule())

        br = const.tile([P, P], BF16, name="br")
        nc.vector.memset(br[:].bitcast(I32), 0)
        ident_f = const.tile([P, P], F32, name="ident_f")
        make_identity(nc, ident_f[:])
        ident_b = const.tile([P, P], BF16, name="ident_b")
        make_identity(nc, ident_b[:])

        x1v = x1.rearrange("(p j) s d -> p j s d", j=4)
        x2v = x2.rearrange("(p j) s d -> p j s d", j=4)
        xt = {}
        w1raw = {}
        w2raw = const.tile([P, G, 4, G * F2], BF16, name="w2raw")

        def load_x_styles(s, n):
            xa = xpool.tile([P, 4, n, D], BF16, name="x1t%d" % s)
            xb = xpool.tile([P, 4, n, D], BF16, name="x2t%d" % s)
            nc.sync.dma_start(out=xa[:], in_=x1v[:, :, s : s + n, :])
            nc.sync.dma_start(out=xb[:], in_=x2v[:, :, s : s + n, :])
            for i in range(n):
                xt[s + i] = (xa, xb, i, n)

        def alloc_w1(h):
            w1raw[h] = w1pool.tile([P, 2, 2, 2 * F1], BF16, name="w1raw", tag="w1raw")

        def load_w1(s0, n):
            h, sl = divmod(s0, 2)
            nc.sync.dma_start(
                out=w1raw[h][:, sl : sl + n, :, :],
                in_=W1[s0 : s0 + n].rearrange("s (u p e) c -> p s u (e c)", u=2, p=P, e=2),
            )

        def load_w2(q):
            for t in range(4):
                nc.sync.dma_start(
                    out=w2raw[:, q, t, :].rearrange("p (s c) -> p s c", s=G),
                    in_=W2[q * G : (q + 1) * G, t * P : (t + 1) * P, :].rearrange("s p c -> p s c"),
                )

        alloc_w1(0)
        alloc_w1(1)
        load_w1(0, 1)
        nc.sync.dma_start(out=br[0:64, :], in_=b1.rearrange("s (t p) -> (s t) p", p=P))
        nc.sync.dma_start(out=br[64:80, :], in_=b2[:, :])
        load_x_styles(0, 1)
        for s in (1, 2):
            load_x_styles(s, 1)
            load_w1(s, 1)
        load_w2(0)
        load_x_styles(3, 1)
        load_w1(3, 1)
        for s in (4, 6):
            load_x_styles(s, 2)
            alloc_w1(s // 2)
            load_w1(s, 1)
            load_w1(s + 1, 1)
        load_w2(1)
        for s in (8, 10):
            load_x_styles(s, 2)
            alloc_w1(s // 2)
            load_w1(s, 2)
        load_w2(2)
        load_x_styles(12, 4)
        for s in (12, 14):
            alloc_w1(s // 2)
            load_w1(s, 2)
        load_w2(3)

        pt = ps_o.tile([P, P], BF16, name="pt", tag="ob")
        nc.tensor.transpose(pt[:], br[:], ident_b[:])
        b1T = const.tile([P, 64], F32, name="b1T")
        b2b = const.tile([P, S * F2], F32, name="b2b")
        def spread_b2(i, copy):
            pb = ps_h.tile([P, 512], F32, name="pb", tag="hb")
            for j in range(4):
                row = 64 + 4 * i + j
                nc.tensor.matmul(
                    pb[:, j * F2 : (j + 1) * F2],
                    lhsT=ident_b[:, row : row + 1].to_broadcast([P, P]),
                    rhs=br[:],
                    start=True,
                    stop=True,
                )
            copy(out=b2b[:, i * 512 : (i + 1) * 512], in_=pb[:])

        w2c = const.tile([P, S * F2], U32, name="w2c", align_bytes=64)
        w2s = const.tile([P, S * F2], U8, name="w2s", align_bytes=64)

        xT, xg, xc, xs = {}, {}, {}, {}
        xwg, xwc, xws = {}, {}, {}
        w1g, w1c, w1s, wb = {}, {}, {}, {}
        hb, hp, hg, hc, hs = {}, {}, {}, {}, {}
        ob, osb, w2g = {}, {}, {}

        def regroup(eng_copy, dst, src, c0, c1):
            eng_copy(
                out=dst[:, c0:c1, :].rearrange("p (c i) t -> p c t i", i=RUN),
                in_=src[:, :, c0:c1].rearrange("p t (c i) -> p c t i", i=RUN),
            )

        def s_cols(s):
            return W1_S_COLS_HEAD.get(s, W1_S_COLS)

        def pe_cols(s):
            return W1_PE_COLS if s >= W1_PE_FIRST else 0

        def w1_src(s):
            h, sl = divmod(s, 2)
            return w1raw[h][:, sl, :, :].rearrange("p u (e c) -> p (u e) c", e=2)

        def regroup_w1_pe(s):
            n = pe_cols(s)
            if n > 0:
                wb[s] = ps_w.tile([P, 4 * n], BF16, name="wb", tag="wb")
                for t in (0, 2):
                    nc.tensor.matmul(
                        wb[s][:].rearrange("p (c t) -> p c t", t=4)[:, :, t : t + 2],
                        lhsT=ident_b[:],
                        rhs=w1_src(s)[:, t : t + 2, F1 - n : F1].rearrange("p t c -> p c t"),
                        start=True,
                        stop=True,
                    )

        def alloc_xw(s):
            xwg[s] = work.tile([P, B + F1, 4], BF16, name="xwg", tag="xwg", align_bytes=64)
            xwc[s] = work.tile([P, B + F1], U32, name="xwc", tag="xwc", bufs=3, align_bytes=64)
            xws[s] = work.tile([P, B + F1], U8, name="xws", tag="xws", bufs=3, align_bytes=64)
            xg[s], w1g[s] = xwg[s][:, 0:B, :], xwg[s][:, B : B + F1, :]
            xc[s], w1c[s] = xwc[s][:, 0:B], xwc[s][:, B : B + F1]
            xs[s], w1s[s] = xws[s][:, 0:B], xws[s][:, B : B + F1]

        def quant_xw(s, c0, c1):
            nc.vector.quantize_mx(
                out=xwc[s][:, c0:c1].bitcast(FP8X4),
                scales=xws[s][:, c0:c1],
                in_=xwg[s][:, c0:c1, :].rearrange("p c t -> p (c t)"),
            )

        def regroup_w1_s(s):
            n = pe_cols(s)
            if n > 0:
                nc.scalar.copy(
                    out=w1g[s][:, F1 - n : F1, :].rearrange("p c t -> p (c t)").bitcast(F32), in_=wb[s][:].bitcast(F32)
                )
            if s_cols(s) > 0:
                regroup(nc.scalar.copy, w1g[s], w1_src(s), F1 - n - s_cols(s), F1 - n)

        def regroup_w1_v(s):
            regroup(nc.vector.tensor_copy, w1g[s], w1_src(s), 0, F1 - s_cols(s) - pe_cols(s))

        def transposes(s):
            sl, n = xt[s][2], xt[s][3]
            xT[s] = []
            for jh in range(2):
                bank = ps_x.tile([P, 2, 256], F32, name="xT", tag="xT")
                xT[s].append(bank)
                for u in range(2):
                    xf = xt[s][u][:].rearrange("p j s d -> p (j s d)").bitcast(F32)
                    for jl in range(2):
                        col = ((2 * jh + jl) * n + sl) * P
                        nc.tensor.transpose(bank[:, u, jl * P : (jl + 1) * P], xf[:, col : col + P], ident_f[:])

        def evac_x(s):
            xgf = xg[s].rearrange("p c t -> p (c t)").bitcast(F32).rearrange("p (c u) -> p c u", u=2)
            for jh in range(2):
                copy = nc.vector.tensor_copy if (s == 0 and jh == 1) else nc.scalar.copy
                copy(out=xgf[:, jh * 256 : (jh + 1) * 256, :], in_=xT[s][jh][:].rearrange("p u c -> p c u"))

        def layer1(s):
            hb[s] = []
            for t in range(4):
                bank = ps_h.tile([P, B], F32, name="hb", tag="hb")
                hb[s].append(bank)
                nc.tensor.matmul_mx(
                    out=bank[:],
                    lhsT=w1c[s][:, t * P : (t + 1) * P].bitcast(FP8X4),
                    lhsT_scale=w1s[s][:, t * P : (t + 1) * P],
                    rhs=xc[s].bitcast(FP8X4),
                    rhs_scale=xs[s],
                    start=True,
                    stop=True,
                )

        def layer1_halves(s):
            hb[s] = []
            for half in range(2):
                for tp in range(2):
                    bank = ps_h.tile([P, 2, 256], F32, name="hb", tag="hb")
                    hb[s].append(bank)
                    for e in range(2):
                        t = 2 * tp + e
                        nc.tensor.matmul_mx(
                            out=bank[:, e, :],
                            lhsT=w1c[s][:, t * P : (t + 1) * P].bitcast(FP8X4),
                            lhsT_scale=w1s[s][:, t * P : (t + 1) * P],
                            rhs=xc[s][:, half * 256 : (half + 1) * 256].bitcast(FP8X4),
                            rhs_scale=xs[s][:, half * 256 : (half + 1) * 256],
                            start=True,
                            stop=True,
                        )

        def evac_h_half(s, half):
            hp[(s, half)] = work.tile([P, 4, 256], BF16, name="hph", tag="hp")
            for t in range(4):
                nc.scalar.activation(
                    out=hp[(s, half)][:, t, :],
                    in_=hb[s][2 * half + t // 2][:, t % 2, :],
                    func=RELU,
                    bias=b1T[:, 4 * s + t : 4 * s + t + 1],
                    scale=1.0,
                )

        def regroup_h_half(s, half):
            hg[(s, half)] = work.tile([P, 256, 4], BF16, name="hgh", tag="hg", align_bytes=64)
            n = RH_S_COLS_END[half]
            if n > 0:
                regroup(nc.scalar.copy, hg[(s, half)], hp[(s, half)], 256 - n, 256)
            regroup(nc.vector.tensor_copy, hg[(s, half)], hp[(s, half)], 0, 256 - n)

        def quant_h_half(s, half):
            hc[(s, half)] = work.tile([P, 256], U32, name="hch", tag="hc", align_bytes=64)
            hs[(s, half)] = work.tile([P, 256], U8, name="hsh", tag="hs", align_bytes=64)
            nc.vector.quantize_mx(
                out=hc[(s, half)][:].bitcast(FP8X4),
                scales=hs[(s, half)][:],
                in_=hg[(s, half)][:].rearrange("p c t -> p (c t)"),
            )

        def layer2_half(s, half):
            obh = ps_x.tile([P, 2, F2], F32, name="obh", tag="xT")
            ob[(s, half)] = obh
            for jl in range(2):
                nc.tensor.matmul_mx(
                    out=obh[:, jl, :],
                    lhsT=hc[(s, half)][:, jl * P : (jl + 1) * P].bitcast(FP8X4),
                    lhsT_scale=hs[(s, half)][:, jl * P : (jl + 1) * P],
                    rhs=w2c[:, s * F2 : (s + 1) * F2].bitcast(FP8X4),
                    rhs_scale=w2s[:, s * F2 : (s + 1) * F2],
                    start=True,
                    stop=True,
                )

        def evac_o_half(s, half):
            osh = work.tile([P, 2, F2], F32, name="osh", tag="osb1", bufs=3)
            nc.vector.tensor_tensor(
                out=osh[:],
                in0=ob[(s, half)][:],
                in1=b2b[:, s * F2 : (s + 1) * F2].unsqueeze(1).to_broadcast([P, 2, F2]),
                op=ADD,
            )
            nc.sync.dma_start(out=outv[:, 2 * half : 2 * half + 2, s, :], in_=osh[:])

        def evac_h(s):
            hp[s] = work.tile([P, 4, B], BF16, name="hp", tag="hp")
            for t in range(4):
                nc.scalar.activation(
                    out=hp[s][:, t, :], in_=hb[s][t][:], func=RELU, bias=b1T[:, 4 * s + t : 4 * s + t + 1], scale=1.0
                )

        def regroup_h(s):
            hg[s] = work.tile([P, B, 4], BF16, name="hg", tag="hg", align_bytes=64)
            n = RH_S_COLS.get(s, 0)
            if n > 0:
                regroup(nc.scalar.copy, hg[s], hp[s], B - n, B)
            regroup(nc.vector.tensor_copy, hg[s], hp[s], 0, B - n)

        def quant_h(s):
            hc[s] = work.tile([P, B], U32, name="hc", tag="hc", align_bytes=64)
            hs[s] = work.tile([P, B], U8, name="hs", tag="hs", align_bytes=64)
            nc.vector.quantize_mx(
                out=hc[s][:].bitcast(FP8X4), scales=hs[s][:], in_=hg[s][:].rearrange("p c t -> p (c t)")
            )

        def regroup_w2(q):
            w2g[q] = work.tile([P, G * F2, 4], BF16, name="w2g", tag="w2g", bufs=1, align_bytes=64)
            regroup(nc.scalar.copy, w2g[q], w2raw[:, q, :, :], G * F2 - W2_S_COLS, G * F2)
            regroup(nc.vector.tensor_copy, w2g[q], w2raw[:, q, :, :], 0, G * F2 - W2_S_COLS)

        def quant_w2(q):
            cols = slice(q * G * F2, (q + 1) * G * F2)
            nc.vector.quantize_mx(
                out=w2c[:, cols].bitcast(FP8X4), scales=w2s[:, cols], in_=w2g[q][:].rearrange("p c t -> p (c t)")
            )

        def layer2(s):
            ob[s] = ps_o.tile([P, 4, F2], F32, name="ob", tag="ob")
            for j in range(4):
                nc.tensor.matmul_mx(
                    out=ob[s][:, j, :],
                    lhsT=hc[s][:, j * P : (j + 1) * P].bitcast(FP8X4),
                    lhsT_scale=hs[s][:, j * P : (j + 1) * P],
                    rhs=w2c[:, s * F2 : (s + 1) * F2].bitcast(FP8X4),
                    rhs_scale=w2s[:, s * F2 : (s + 1) * F2],
                    start=True,
                    stop=True,
                )

        outv = out.rearrange("(p j) s f -> p j s f", j=4)

        def evac_o(s):
            for s0, n in STORES:
                if s0 <= s < s0 + n:
                    if s == s0:
                        osb[s0] = work.tile([P, 4, n, F2], F32, name="osb%d" % n, tag="osb%d" % n, bufs=OSB_BUFS[n])
                    nc.vector.tensor_tensor(
                        out=osb[s0][:, :, s - s0, :],
                        in0=ob[s][:],
                        in1=b2b[:, s * F2 : (s + 1) * F2].unsqueeze(1).to_broadcast([P, 4, F2]),
                        op=ADD,
                    )
                    if s == s0 + n - 1:
                        nc.sync.dma_start(out=outv[:, :, s0 : s0 + n, :], in_=osb[s0][:])

        def on(s):
            return 0 <= s < S

        spread_b2(0, nc.scalar.copy)
        spread_b2(1, nc.scalar.copy)
        spread_b2(3, nc.scalar.copy)
        alloc_xw(0)
        regroup_w1_s(0)
        regroup_w1_v(0)
        nc.vector.tensor_copy(out=b1T[:], in_=pt[:, 0:64])
        quant_xw(0, B, B + F1)
        transposes(0)
        evac_x(0)
        spread_b2(2, nc.vector.tensor_copy)
        quant_xw(0, 0, B)
        transposes(1)
        layer1(0)
        alloc_xw(1)
        evac_x(1)
        regroup_w1_s(1)
        regroup_w1_v(1)
        for k in range(0, S):
            if on(k + 2):
                transposes(k + 2)
                regroup_w1_pe(k + 2)
            if on(k + 1):
                quant_xw(k + 1, 0, B + F1)
            if on(k - 1) and (k - 1) % G == 0:
                quant_w2((k - 1) // G)
            if on(k - 1):
                layer2(k - 1)
            if on(k) and k != LAST:
                evac_h(k)
            if k == LAST:
                evac_h_half(k, 0)
                evac_h_half(k, 1)
            if on(k + 1):
                if k + 1 == LAST:
                    layer1_halves(k + 1)
                else:
                    layer1(k + 1)
            if on(k + 2):
                alloc_xw(k + 2)
                evac_x(k + 2)
                regroup_w1_s(k + 2)
            if on(k + 2):
                regroup_w1_v(k + 2)
            if on(k) and k != LAST:
                regroup_h(k)
            if k == LAST:
                regroup_h_half(k, 0)
            if on(k - 1):
                evac_o(k - 1)
            if on(k) and k != LAST:
                quant_h(k)
            if on(k) and k % G == 0:
                regroup_w2(k // G)
        quant_h_half(LAST, 0)
        layer2_half(LAST, 0)
        regroup_h_half(LAST, 1)
        quant_h_half(LAST, 1)
        layer2_half(LAST, 1)
        evac_o_half(LAST, 0)
        evac_o_half(LAST, 1)
